import numpy as np
import ml_dtypes


def mxq(x, axis, fmt="e4m3"):
    dtype, down = {"e4m3": (ml_dtypes.float8_e4m3fn, 7), "e5m2": (ml_dtypes.float8_e5m2, 14)}[fmt]
    v = np.moveaxis(np.asarray(x, np.float32).astype(ml_dtypes.bfloat16).astype(np.float64), axis, -1)
    blocks = v.reshape(v.shape[:-1] + (-1, 32))
    amax = np.abs(blocks).max(-1, keepdims=True)
    byte = np.maximum(np.where(amax > 0, np.frexp(amax)[1] - 1 + 127, 0) - down, 1)
    scale = np.exp2(byte - 127.0)
    codes = (blocks / scale).astype(np.float32).astype(dtype).astype(np.float64)
    return np.moveaxis((codes * scale).reshape(v.shape), -1, axis)


WIDE = False


def mx_kscale(k):
    if not WIDE:
        return np.ones(k)
    levels = np.array([10, -10, 5, -5, 0])
    a = np.random.permutation(np.resize(levels, k // 512 * 4)).reshape(k // 512, 4)
    idx = np.arange(k)
    return np.exp2(a[idx // 512, idx % 128 // 32])


BF16 = ml_dtypes.bfloat16


def bf(x):
    return np.asarray(x, np.float32).astype(BF16)


def f64(x):
    return np.asarray(x).astype(np.float64)


B, T, D, H, HD, F = 2, 64, 512, 16, 64, 2048
A = H * HD
EPS = 1e-5
ERF_H = 0.5
ERF_N = 14


def layernorm(x, g, b):
    mu = np.mean(x, axis=-1, keepdims=True)
    var = np.mean(np.square(x - mu), axis=-1, keepdims=True)
    return (x - mu) / np.sqrt(var + EPS) * g + b


def erf(z):
    acc = np.zeros_like(z)
    for n in range(ERF_N):
        tn = (n + 0.5) * ERF_H
        acc = acc + np.exp(-tn * tn) / (tn * tn + z * z)
    return np.tanh(np.pi * z / ERF_H) - 2.0 * ERF_H * z * np.exp(-z * z) / np.pi * acc


def gelu_erf(v):
    return 0.5 * v * (1.0 + erf(v / np.sqrt(2.0)))


def setup_inputs():
    s, t = mx_kscale(A), mx_kscale(D)
    return {"attn": bf(np.random.standard_normal((B, T, A)) * 0.25 * s),
            "x": bf(np.random.standard_normal((B, T, D)) + 0.5 * np.random.standard_normal((B, T, 1))),
            "w_out": bf(np.random.standard_normal((A, D)) * 2.0 / np.sqrt(A) / s[:, None]),
            "b_out": bf(0.1 * np.random.standard_normal(D)),
            "ln2_g": bf((1.0 + 0.1 * np.random.standard_normal(D)) * t),
            "ln2_b": bf(0.1 * np.random.standard_normal(D) * t),
            "w1": bf(np.random.standard_normal((D, F)) / np.sqrt(D) / t[:, None]),
            "b1": bf(0.2 * np.random.standard_normal(F))}


def reference(attn, x, w_out, b_out, ln2_g, ln2_b, w1, b1):
    x_mid = f64(x) + ((mxq(f64(attn), 2, "e4m3") @ mxq(f64(w_out), 0, "e4m3")) + f64(b_out))
    h2 = layernorm(x_mid, f64(ln2_g), f64(ln2_b))
    hid = gelu_erf((mxq(h2, 2, "e4m3") @ mxq(f64(w1), 0, "e4m3")) + f64(b1))
    return x_mid, hid

@@ -1,0 +1,252 @@
+from contextlib import ExitStack
+
+import concourse.mybir as mybir
+from concourse.masks import make_identity
+
+BF16 = mybir.dt.bfloat16
+F32 = mybir.dt.float32
+U32 = mybir.dt.uint32
+U8 = mybir.dt.uint8
+FP8X4 = mybir.dt.float8_e4m3fn_x4
+ACT = mybir.ActivationFunctionType
+ALU = mybir.AluOpType
+
+P = 128
+PACK = 4
+K_PASS = P * PACK
+A = 1024
+D = 512
+F = 2048
+EPS = 1e-5
+PASSES_1 = A // K_PASS
+CHUNK = 512
+CHUNKS_2 = F // CHUNK
+SLICES = CHUNK // P
+RUN = 4
+VECTOR_COLS = 256
+
+FLOPS = 2 * P * A * D + 2 * P * D * F
+
+
+def regroup(nc, grouped, raw):
+    src = raw[:].rearrange("p t (c i) -> p c t i", i=RUN)
+    dst = grouped[:].rearrange("p (c i) t -> p c t i", i=RUN)
+    split = VECTOR_COLS // RUN
+    nc.vector.tensor_copy(out=dst[:, :split], in_=src[:, :split])
+    nc.scalar.copy(out=dst[:, split:], in_=src[:, split:])
+
+
+def quantise(nc, codes, scales, grouped):
+    nc.vector.quantize_mx(
+        out=codes.bitcast(FP8X4),
+        scales=scales,
+        in_=grouped.rearrange("p c t -> p (c t)"),
+    )
+
+
+def tile_transformerblock_pb_s_kernel(
+    tc, attn, x, w_out, b_out, ln2_g, ln2_b, w1, b1, out_0, out_1
+):
+    nc = tc.nc
+    with ExitStack() as ctx:
+        keep = ctx.enter_context(tc.tile_pool(name="keep", bufs=1))
+        psum = ctx.enter_context(tc.psum_pool(name="psum", bufs=8))
+
+        ident_f32 = keep.tile([P, P], F32, name="ident_f32")
+        make_identity(nc, ident_f32[:])
+        ident_bf16 = keep.tile([P, P], BF16, name="ident_bf16")
+        make_identity(nc, ident_bf16[:])
+        ones_bf16 = keep.tile([P, P], BF16, name="ones_bf16")
+        nc.vector.memset(ones_bf16[:], 1.0)
+        neg_half = keep.tile([P, 1], F32, name="neg_half")
+        nc.vector.memset(neg_half[:], -0.5)
+        bias_rows = keep.tile([P, D], BF16, name="bias_rows")
+        nc.vector.memset(bias_rows[:], 0.0)
+        vec_rows = keep.tile([P, P], BF16, name="vec_rows")
+        nc.vector.memset(vec_rows[:], 0.0)
+        warm = keep.tile([P, 1], F32, name="warm")
+        nc.vector.memset(warm[:], 0.0)
+
+        attn_sb = keep.tile([P, A], BF16, name="attn_sb")
+        nc.sync.dma_start(out=attn_sb[:], in_=attn.rearrange("b t a -> (b t) a"))
+        x_sb = keep.tile([P, D], BF16, name="x_sb")
+        nc.scalar.dma_start(out=x_sb[:], in_=x.rearrange("b t d -> (b t) d"))
+        nc.scalar.dma_start(out=bias_rows[0:1, :], in_=b_out.rearrange("(o d) -> o d", o=1))
+        wo_raw = []
+        for g in range(PASSES_1):
+            raw = keep.tile([P, PACK, D], BF16, name="wo_raw%d" % g)
+            nc.sync.dma_start(
+                out=raw[:].rearrange("q (u e) c -> q u (e c)", e=2),
+                in_=w_out[g * K_PASS : (g + 1) * K_PASS, :].rearrange(
+                    "(u q e) c -> q u (e c)", u=2, e=2
+                ),
+            )
+            wo_raw.append(raw)
+        G_ROW, B_ROW, B1_ROW = 0, D // P, 2 * (D // P)
+        VEC_ROWS = B1_ROW + F // P
+        nc.scalar.dma_start(
+            out=vec_rows[G_ROW:B_ROW, :], in_=ln2_g.rearrange("(r c) -> r c", c=P)
+        )
+        nc.scalar.dma_start(
+            out=vec_rows[B_ROW:B1_ROW, :], in_=ln2_b.rearrange("(r c) -> r c", c=P)
+        )
+        nc.scalar.dma_start(
+            out=vec_rows[B1_ROW:VEC_ROWS, :], in_=b1.rearrange("(r c) -> r c", c=P)
+        )
+        w1_raw = []
+        for c in range(CHUNKS_2):
+            raw = keep.tile([P, PACK, CHUNK], BF16, name="w1_raw%d" % c)
+            nc.sync.dma_start(
+                out=raw[:],
+                in_=w1[:, c * CHUNK : (c + 1) * CHUNK].rearrange("(t p) n -> p t n", p=P),
+            )
+            w1_raw.append(raw)
+
+        warm_out = keep.tile([P, 1], F32, name="warm_out")
+        nc.scalar.activation(out=warm_out[:], in_=warm[:], func=ACT.Gelu)
+
+        attn_words = attn_sb[:].bitcast(F32)
+        attnT_ps = psum.tile([P, PASSES_1, 2, P], F32, tag="bank", name="attnT_ps")
+        for g in range(PASSES_1):
+            for u in range(2):
+                first = (2 * g + u) * P
+                nc.tensor.transpose(
+                    attnT_ps[:, g, u, :], attn_words[:, first : first + P], ident_f32[:]
+                )
+        attn_grp = keep.tile([P, PASSES_1 * P, PACK], BF16, name="attn_grp", align_bytes=64)
+        nc.scalar.copy(
+            out=attn_grp[:]
+            .rearrange("p r t -> p (r t)")
+            .bitcast(F32)
+            .rearrange("p (g r u) -> p g r u", g=PASSES_1, u=2),
+            in_=attnT_ps[:].rearrange("p g u r -> p g r u"),
+        )
+        attn_codes = keep.tile([P, PASSES_1 * P], U32, name="attn_codes", align_bytes=64)
+        attn_scales = keep.tile([P, PASSES_1 * P], U8, name="attn_scales", align_bytes=64)
+        quantise(nc, attn_codes[:], attn_scales[:], attn_grp[:])
+
+        xb_ps = psum.tile([P, D], F32, tag="bank", name="xb_ps")
+        nc.tensor.matmul(xb_ps[:], lhsT=ident_bf16[:], rhs=x_sb[:], start=True, stop=False)
+        nc.tensor.matmul(xb_ps[:], lhsT=ones_bf16[:], rhs=bias_rows[:], start=False, stop=True)
+        xb_sb = keep.tile([P, D], F32, name="xb_sb")
+        nc.scalar.copy(out=xb_sb[:], in_=xb_ps[:])
+
+        vecT_ps = psum.tile([P, P], BF16, tag="bank", name="vecT_ps")
+        nc.tensor.transpose(vecT_ps[:], vec_rows[:], ident_bf16[:])
+        vec_cols = keep.tile([P, VEC_ROWS], F32, name="vec_cols")
+        nc.vector.tensor_copy(out=vec_cols[:], in_=vecT_ps[:, 0:VEC_ROWS])
+
+        wo_codes = keep.tile([P, PASSES_1, D], U32, name="wo_codes", align_bytes=64)
+        wo_scales = keep.tile([P, PASSES_1, D], U8, name="wo_scales", align_bytes=64)
+        for g in range(PASSES_1):
+            grouped = keep.tile([P, D, PACK], BF16, name="wo_grp%d" % g, align_bytes=64)
+            regroup(nc, grouped, wo_raw[g])
+            quantise(nc, wo_codes[:, g, :], wo_scales[:, g, :], grouped[:])
+
+        acc1_ps = psum.tile([P, D], F32, tag="bank", name="acc1_ps")
+        for g in range(PASSES_1):
+            tokens = slice(g * P, (g + 1) * P)
+            nc.tensor.matmul_mx(
+                out=acc1_ps[:],
+                lhsT=attn_codes[:, tokens].bitcast(FP8X4),
+                lhsT_scale=attn_scales[:, tokens],
+                rhs=wo_codes[:, g, :].bitcast(FP8X4),
+                rhs_scale=wo_scales[:, g, :],
+                start=(g == 0),
+                stop=(g == PASSES_1 - 1),
+            )
+        x_mid = keep.tile([P, D], F32, name="x_mid")
+        nc.vector.tensor_tensor(out=x_mid[:], in0=acc1_ps[:], in1=xb_sb[:], op=ALU.add)
+        nc.sync.dma_start(out=out_0.rearrange("b t d -> (b t) d"), in_=x_mid[:])
+
+        stats = keep.tile([P, 6], F32, name="stats")
+        nc.vector.bn_stats(out=stats[:], in_=x_mid[:])
+        mean_var = keep.tile([P, 2], F32, name="mean_var")
+        nc.vector.bn_aggr(out=mean_var[:], in_=stats[:])
+        var_eps = keep.tile([P, 1], F32, name="var_eps")
+        nc.vector.tensor_scalar_add(out=var_eps[:], in0=mean_var[:, 1:2], scalar1=EPS)
+        rstd = keep.tile([P, 1], F32, name="rstd")
+        nc.gpsimd.tensor_tensor(out=rstd[:], in0=var_eps[:], in1=neg_half[:], op=ALU.pow)
+        z = keep.tile([P, D], F32, name="z")
+        nc.vector.tensor_scalar(
+            out=z[:],
+            in0=x_mid[:],
+            scalar1=mean_var[:, 0:1],
+            scalar2=rstd[:],
+            op0=ALU.subtract,
+            op1=ALU.mult,
+        )
+
+        h2_planes = keep.tile([P, PACK, P], BF16, name="h2_planes")
+        zT_ps = [
+            psum.tile([P, PACK // 2, P], F32, tag="bank", name="zT_ps%d" % half)
+            for half in range(2)
+        ]
+        for t in range(PACK):
+            nc.tensor.transpose(
+                zT_ps[t // 2][:, t % 2, :], z[:, t * P : (t + 1) * P], ident_f32[:]
+            )
+        for t in range(PACK):
+            gain = vec_cols[:, G_ROW + t : G_ROW + t + 1]
+            bias = vec_cols[:, B_ROW + t : B_ROW + t + 1]
+            if t // 2 == 0:
+                nc.vector.tensor_scalar(
+                    out=h2_planes[:, t, :],
+                    in0=zT_ps[0][:, t % 2, :],
+                    scalar1=gain,
+                    scalar2=bias,
+                    op0=ALU.mult,
+                    op1=ALU.add,
+                )
+            else:
+                nc.scalar.activation(
+                    out=h2_planes[:, t, :],
+                    in_=zT_ps[1][:, t % 2, :],
+                    func=ACT.Identity,
+                    scale=gain,
+                    bias=bias,
+                )
+        h2_grp = keep.tile([P, P, PACK], BF16, name="h2_grp", align_bytes=64)
+        nc.vector.tensor_copy(
+            out=h2_grp[:].rearrange("p (c i) t -> p c t i", i=RUN),
+            in_=h2_planes[:].rearrange("p t (c i) -> p c t i", i=RUN),
+        )
+        h2_codes = keep.tile([P, P], U32, name="h2_codes", align_bytes=64)
+        h2_scales = keep.tile([P, P], U8, name="h2_scales", align_bytes=64)
+        quantise(nc, h2_codes[:], h2_scales[:], h2_grp[:])
+
+        w1_codes = keep.tile([P, CHUNKS_2, CHUNK], U32, name="w1_codes", align_bytes=64)
+        w1_scales = keep.tile([P, CHUNKS_2, CHUNK], U8, name="w1_scales", align_bytes=64)
+        hid_rows = out_1.rearrange("b t f -> (b t) f")
+        for c in range(CHUNKS_2):
+            grouped = keep.tile([P, CHUNK, PACK], BF16, name="w1_grp%d" % c, align_bytes=64)
+            regroup(nc, grouped, w1_raw[c])
+            quantise(nc, w1_codes[:, c, :], w1_scales[:, c, :], grouped[:])
+
+            hidT_ps = psum.tile([P, SLICES, P], F32, tag="bank", name="hidT_ps%d" % c)
+            for s in range(SLICES):
+                feats = slice(s * P, (s + 1) * P)
+                nc.tensor.matmul_mx(
+                    out=hidT_ps[:, s, :],
+                    lhsT=w1_codes[:, c, feats].bitcast(FP8X4),
+                    lhsT_scale=w1_scales[:, c, feats],
+                    rhs=h2_codes[:].bitcast(FP8X4),
+                    rhs_scale=h2_scales[:],
+                    start=True,
+                    stop=True,
+                )
+            geluT = keep.tile([P, SLICES, P], F32, name="geluT%d" % c)
+            for s in range(SLICES):
+                row = B1_ROW + c * SLICES + s
+                nc.scalar.activation(
+                    out=geluT[:, s, :],
+                    in_=hidT_ps[:, s, :],
+                    func=ACT.Gelu,
+                    bias=vec_cols[:, row : row + 1],
+                )
+            hid_ps = psum.tile([P, CHUNK], F32, tag="bank", name="hid_ps%d" % c)
+            for s in range(SLICES):
+                nc.tensor.transpose(hid_ps[:, s * P : (s + 1) * P], geluT[:, s, :], ident_f32[:])
+            hid_sb = keep.tile([P, CHUNK], F32, name="hid_sb%d" % c)
+            nc.vector.tensor_copy(out=hid_sb[:], in_=hid_ps[:])
+            nc.sync.dma_start(out=hid_rows[:, c * CHUNK : (c + 1) * CHUNK], in_=hid_sb[:])

@@ -21,18 +21,33 @@ EPS = 1e-5
 PASSES_1 = A // K_PASS
 CHUNK = 512
 CHUNKS_2 = F // CHUNK
-SLICES = CHUNK // P
 RUN = 4
-VECTOR_COLS = 256
+VECTOR_COLS_WO = 384
+VECTOR_COLS_W1 = 256
+G_ROW = 0
+B_ROW = D // P
+B1_ROW = 2 * (D // P)
+VEC_ROWS = B1_ROW + F // P
+BANK_BF16 = 1024
 
 FLOPS = 2 * P * A * D + 2 * P * D * F
 
 
-def regroup(nc, grouped, raw):
+def regroup_views(grouped, raw):
     src = raw[:].rearrange("p t (c i) -> p c t i", i=RUN)
     dst = grouped[:].rearrange("p (c i) t -> p c t i", i=RUN)
-    split = VECTOR_COLS // RUN
+    return dst, src
+
+
+def regroup_on_vector(nc, grouped, raw, vector_cols):
+    dst, src = regroup_views(grouped, raw)
+    split = vector_cols // RUN
     nc.vector.tensor_copy(out=dst[:, :split], in_=src[:, :split])
+
+
+def regroup_on_scalar(nc, grouped, raw, vector_cols):
+    dst, src = regroup_views(grouped, raw)
+    split = vector_cols // RUN
     nc.scalar.copy(out=dst[:, split:], in_=src[:, split:])
 
 
@@ -51,59 +66,84 @@ def tile_transformerblock_pb_s_kernel(
     with ExitStack() as ctx:
         keep = ctx.enter_context(tc.tile_pool(name="keep", bufs=1))
         psum = ctx.enter_context(tc.psum_pool(name="psum", bufs=8))
+        ctx.enter_context(tc.manual_schedule())
 
-        ident_f32 = keep.tile([P, P], F32, name="ident_f32")
-        make_identity(nc, ident_f32[:])
         ident_bf16 = keep.tile([P, P], BF16, name="ident_bf16")
         make_identity(nc, ident_bf16[:])
-        ones_bf16 = keep.tile([P, P], BF16, name="ones_bf16")
-        nc.vector.memset(ones_bf16[:], 1.0)
-        neg_half = keep.tile([P, 1], F32, name="neg_half")
-        nc.vector.memset(neg_half[:], -0.5)
+        ident_f32 = keep.tile([P, P], F32, name="ident_f32")
+        make_identity(nc, ident_f32[:])
         bias_rows = keep.tile([P, D], BF16, name="bias_rows")
         nc.vector.memset(bias_rows[:], 0.0)
         vec_rows = keep.tile([P, P], BF16, name="vec_rows")
         nc.vector.memset(vec_rows[:], 0.0)
+        ones_bf16 = keep.tile([P, P], BF16, name="ones_bf16")
+        nc.vector.memset(ones_bf16[:], 1.0)
+        neg_half = keep.tile([P, 1], F32, name="neg_half")
+        nc.vector.memset(neg_half[:], -0.5)
         warm = keep.tile([P, 1], F32, name="warm")
         nc.vector.memset(warm[:], 0.0)
 
-        attn_sb = keep.tile([P, A], BF16, name="attn_sb")
-        nc.sync.dma_start(out=attn_sb[:], in_=attn.rearrange("b t a -> (b t) a"))
         x_sb = keep.tile([P, D], BF16, name="x_sb")
         nc.scalar.dma_start(out=x_sb[:], in_=x.rearrange("b t d -> (b t) d"))
         nc.scalar.dma_start(out=bias_rows[0:1, :], in_=b_out.rearrange("(o d) -> o d", o=1))
-        wo_raw = []
-        for g in range(PASSES_1):
-            raw = keep.tile([P, PACK, D], BF16, name="wo_raw%d" % g)
+        attn_sb = keep.tile([P, A], BF16, name="attn_sb")
+        wo_raw = [keep.tile([P, PACK, D], BF16, name="wo_raw%d" % g) for g in range(PASSES_1)]
+
+        def load_w_out(g):
             nc.sync.dma_start(
-                out=raw[:].rearrange("q (u e) c -> q u (e c)", e=2),
+                out=wo_raw[g][:].rearrange("q (u e) c -> q u (e c)", e=2),
                 in_=w_out[g * K_PASS : (g + 1) * K_PASS, :].rearrange(
                     "(u q e) c -> q u (e c)", u=2, e=2
                 ),
             )
-            wo_raw.append(raw)
-        G_ROW, B_ROW, B1_ROW = 0, D // P, 2 * (D // P)
-        VEC_ROWS = B1_ROW + F // P
+
+        load_w_out(0)
+        nc.sync.dma_start(out=attn_sb[:], in_=attn.rearrange("b t a -> (b t) a"))
+        load_w_out(1)
+        nc.scalar.dma_start(
+            out=vec_rows[B1_ROW:VEC_ROWS, :], in_=b1.rearrange("(r c) -> r c", c=P)
+        )
         nc.scalar.dma_start(
             out=vec_rows[G_ROW:B_ROW, :], in_=ln2_g.rearrange("(r c) -> r c", c=P)
         )
         nc.scalar.dma_start(
             out=vec_rows[B_ROW:B1_ROW, :], in_=ln2_b.rearrange("(r c) -> r c", c=P)
         )
-        nc.scalar.dma_start(
-            out=vec_rows[B1_ROW:VEC_ROWS, :], in_=b1.rearrange("(r c) -> r c", c=P)
-        )
-        w1_raw = []
+        w1_raw = [keep.tile([P, PACK, CHUNK], BF16, name="w1_raw%d" % c) for c in range(CHUNKS_2)]
         for c in range(CHUNKS_2):
-            raw = keep.tile([P, PACK, CHUNK], BF16, name="w1_raw%d" % c)
             nc.sync.dma_start(
-                out=raw[:],
+                out=w1_raw[c][:],
                 in_=w1[:, c * CHUNK : (c + 1) * CHUNK].rearrange("(t p) n -> p t n", p=P),
             )
-            w1_raw.append(raw)
 
         warm_out = keep.tile([P, 1], F32, name="warm_out")
         nc.scalar.activation(out=warm_out[:], in_=warm[:], func=ACT.Gelu)
+
+        wo_grp = [
+            keep.tile([P, D, PACK], BF16, name="wo_grp%d" % g, align_bytes=64)
+            for g in range(PASSES_1)
+        ]
+        wo_codes = keep.tile([P, PASSES_1, D], U32, name="wo_codes", align_bytes=64)
+        wo_scales = keep.tile([P, PASSES_1, D], U8, name="wo_scales", align_bytes=64)
+        w1_grp = [
+            keep.tile([P, CHUNK, PACK], BF16, name="w1_grp%d" % c, align_bytes=64)
+            for c in range(CHUNKS_2)
+        ]
+        w1_codes = keep.tile([P, CHUNKS_2, CHUNK], U32, name="w1_codes", align_bytes=64)
+        w1_scales = keep.tile([P, CHUNKS_2, CHUNK], U8, name="w1_scales", align_bytes=64)
+
+        def quantise_w_out(g):
+            quantise(nc, wo_codes[:, g, :], wo_scales[:, g, :], wo_grp[g][:])
+
+        def quantise_w1(c):
+            quantise(nc, w1_codes[:, c, :], w1_scales[:, c, :], w1_grp[c][:])
+
+        xb_ps = psum.tile([P, D], F32, tag="bank", name="xb_ps")
+        nc.tensor.matmul(xb_ps[:], lhsT=ident_bf16[:], rhs=x_sb[:], start=True, stop=False)
+        nc.tensor.matmul(xb_ps[:], lhsT=ones_bf16[:], rhs=bias_rows[:], start=False, stop=True)
+
+        regroup_on_vector(nc, wo_grp[0], wo_raw[0], VECTOR_COLS_WO)
+        regroup_on_scalar(nc, wo_grp[0], wo_raw[0], VECTOR_COLS_WO)
 
         attn_words = attn_sb[:].bitcast(F32)
         attnT_ps = psum.tile([P, PASSES_1, 2, P], F32, tag="bank", name="attnT_ps")
@@ -121,27 +161,36 @@ def tile_transformerblock_pb_s_kernel(
             .rearrange("p (g r u) -> p g r u", g=PASSES_1, u=2),
             in_=attnT_ps[:].rearrange("p g u r -> p g r u"),
         )
-        attn_codes = keep.tile([P, PASSES_1 * P], U32, name="attn_codes", align_bytes=64)
-        attn_scales = keep.tile([P, PASSES_1 * P], U8, name="attn_scales", align_bytes=64)
-        quantise(nc, attn_codes[:], attn_scales[:], attn_grp[:])
-
-        xb_ps = psum.tile([P, D], F32, tag="bank", name="xb_ps")
-        nc.tensor.matmul(xb_ps[:], lhsT=ident_bf16[:], rhs=x_sb[:], start=True, stop=False)
-        nc.tensor.matmul(xb_ps[:], lhsT=ones_bf16[:], rhs=bias_rows[:], start=False, stop=True)
-        xb_sb = keep.tile([P, D], F32, name="xb_sb")
-        nc.scalar.copy(out=xb_sb[:], in_=xb_ps[:])
+        quantise_w_out(0)
 
         vecT_ps = psum.tile([P, P], BF16, tag="bank", name="vecT_ps")
         nc.tensor.transpose(vecT_ps[:], vec_rows[:], ident_bf16[:])
-        vec_cols = keep.tile([P, VEC_ROWS], F32, name="vec_cols")
-        nc.vector.tensor_copy(out=vec_cols[:], in_=vecT_ps[:, 0:VEC_ROWS])
+        b1_cols = keep.tile([P, F // P], BF16, name="b1_cols")
+        nc.vector.tensor_copy(out=b1_cols[:], in_=vecT_ps[:, B1_ROW:VEC_ROWS])
+        ln_cols = keep.tile([P, B1_ROW], F32, name="ln_cols")
+        nc.vector.tensor_copy(out=ln_cols[:], in_=vecT_ps[:, 0:B1_ROW])
 
-        wo_codes = keep.tile([P, PASSES_1, D], U32, name="wo_codes", align_bytes=64)
-        wo_scales = keep.tile([P, PASSES_1, D], U8, name="wo_scales", align_bytes=64)
-        for g in range(PASSES_1):
-            grouped = keep.tile([P, D, PACK], BF16, name="wo_grp%d" % g, align_bytes=64)
-            regroup(nc, grouped, wo_raw[g])
-            quantise(nc, wo_codes[:, g, :], wo_scales[:, g, :], grouped[:])
+        b1_all = keep.tile([P, F], BF16, name="b1_all")
+        b1_ps = [
+            psum.tile([P, BANK_BF16], BF16, tag="bank", name="b1_ps%d" % half)
+            for half in range(F // BANK_BF16)
+        ]
+        for r in range(F // P):
+            first = (r * P) % BANK_BF16
+            nc.tensor.transpose(
+                b1_ps[r * P // BANK_BF16][:, first : first + P],
+                b1_cols[:, r : r + 1].to_broadcast([P, P]),
+                ident_bf16[:],
+            )
+
+        regroup_on_vector(nc, wo_grp[1], wo_raw[1], VECTOR_COLS_WO)
+        regroup_on_scalar(nc, wo_grp[1], wo_raw[1], VECTOR_COLS_WO)
+        attn_codes = keep.tile([P, PASSES_1 * P], U32, name="attn_codes", align_bytes=64)
+        attn_scales = keep.tile([P, PASSES_1 * P], U8, name="attn_scales", align_bytes=64)
+        quantise(nc, attn_codes[:], attn_scales[:], attn_grp[:])
+        quantise_w_out(1)
+        xb_sb = keep.tile([P, D], F32, name="xb_sb")
+        nc.scalar.copy(out=xb_sb[:], in_=xb_ps[:])
 
         acc1_ps = psum.tile([P, D], F32, tag="bank", name="acc1_ps")
         for g in range(PASSES_1):
@@ -155,6 +204,15 @@ def tile_transformerblock_pb_s_kernel(
                 start=(g == 0),
                 stop=(g == PASSES_1 - 1),
             )
+        regroup_on_vector(nc, w1_grp[0], w1_raw[0], VECTOR_COLS_W1)
+        regroup_on_scalar(nc, w1_grp[0], w1_raw[0], VECTOR_COLS_W1)
+        for half in range(F // BANK_BF16):
+            nc.scalar.copy(
+                out=b1_all[:, half * BANK_BF16 : (half + 1) * BANK_BF16], in_=b1_ps[half][:]
+            )
+        regroup_on_scalar(nc, w1_grp[1], w1_raw[1], VECTOR_COLS_W1)
+        regroup_on_scalar(nc, w1_grp[2], w1_raw[2], VECTOR_COLS_W1)
+
         x_mid = keep.tile([P, D], F32, name="x_mid")
         nc.vector.tensor_tensor(out=x_mid[:], in0=acc1_ps[:], in1=xb_sb[:], op=ALU.add)
         nc.sync.dma_start(out=out_0.rearrange("b t d -> (b t) d"), in_=x_mid[:])
@@ -167,6 +225,7 @@ def tile_transformerblock_pb_s_kernel(
         nc.vector.tensor_scalar_add(out=var_eps[:], in0=mean_var[:, 1:2], scalar1=EPS)
         rstd = keep.tile([P, 1], F32, name="rstd")
         nc.gpsimd.tensor_tensor(out=rstd[:], in0=var_eps[:], in1=neg_half[:], op=ALU.pow)
+        quantise_w1(0)
         z = keep.tile([P, D], F32, name="z")
         nc.vector.tensor_scalar(
             out=z[:],
@@ -177,7 +236,6 @@ def tile_transformerblock_pb_s_kernel(
             op1=ALU.mult,
         )
 
-        h2_planes = keep.tile([P, PACK, P], BF16, name="h2_planes")
         zT_ps = [
             psum.tile([P, PACK // 2, P], F32, tag="bank", name="zT_ps%d" % half)
             for half in range(2)
@@ -186,9 +244,11 @@ def tile_transformerblock_pb_s_kernel(
             nc.tensor.transpose(
                 zT_ps[t // 2][:, t % 2, :], z[:, t * P : (t + 1) * P], ident_f32[:]
             )
+        regroup_on_vector(nc, w1_grp[1], w1_raw[1], VECTOR_COLS_W1)
+        h2_planes = keep.tile([P, PACK, P], BF16, name="h2_planes")
         for t in range(PACK):
-            gain = vec_cols[:, G_ROW + t : G_ROW + t + 1]
-            bias = vec_cols[:, B_ROW + t : B_ROW + t + 1]
+            gain = ln_cols[:, G_ROW + t : G_ROW + t + 1]
+            bias = ln_cols[:, B_ROW + t : B_ROW + t + 1]
             if t // 2 == 0:
                 nc.vector.tensor_scalar(
                     out=h2_planes[:, t, :],
@@ -206,47 +266,47 @@ def tile_transformerblock_pb_s_kernel(
                     scale=gain,
                     bias=bias,
                 )
+        regroup_on_scalar(nc, w1_grp[3], w1_raw[3], VECTOR_COLS_W1)
         h2_grp = keep.tile([P, P, PACK], BF16, name="h2_grp", align_bytes=64)
-        nc.vector.tensor_copy(
-            out=h2_grp[:].rearrange("p (c i) t -> p c t i", i=RUN),
-            in_=h2_planes[:].rearrange("p t (c i) -> p c t i", i=RUN),
-        )
+        regroup_on_vector(nc, h2_grp, h2_planes, P)
+        quantise_w1(1)
         h2_codes = keep.tile([P, P], U32, name="h2_codes", align_bytes=64)
         h2_scales = keep.tile([P, P], U8, name="h2_scales", align_bytes=64)
         quantise(nc, h2_codes[:], h2_scales[:], h2_grp[:])
 
-        w1_codes = keep.tile([P, CHUNKS_2, CHUNK], U32, name="w1_codes", align_bytes=64)
-        w1_scales = keep.tile([P, CHUNKS_2, CHUNK], U8, name="w1_scales", align_bytes=64)
         hid_rows = out_1.rearrange("b t f -> (b t) f")
-        for c in range(CHUNKS_2):
-            grouped = keep.tile([P, CHUNK, PACK], BF16, name="w1_grp%d" % c, align_bytes=64)
-            regroup(nc, grouped, w1_raw[c])
-            quantise(nc, w1_codes[:, c, :], w1_scales[:, c, :], grouped[:])
+        hid_ps = [
+            psum.tile([P, CHUNK], F32, tag="bank", name="hid_ps%d" % c) for c in range(CHUNKS_2)
+        ]
 
-            hidT_ps = psum.tile([P, SLICES, P], F32, tag="bank", name="hidT_ps%d" % c)
-            for s in range(SLICES):
-                feats = slice(s * P, (s + 1) * P)
-                nc.tensor.matmul_mx(
-                    out=hidT_ps[:, s, :],
-                    lhsT=w1_codes[:, c, feats].bitcast(FP8X4),
-                    lhsT_scale=w1_scales[:, c, feats],
-                    rhs=h2_codes[:].bitcast(FP8X4),
-                    rhs_scale=h2_scales[:],
-                    start=True,
-                    stop=True,
-                )
-            geluT = keep.tile([P, SLICES, P], F32, name="geluT%d" % c)
-            for s in range(SLICES):
-                row = B1_ROW + c * SLICES + s
-                nc.scalar.activation(
-                    out=geluT[:, s, :],
-                    in_=hidT_ps[:, s, :],
-                    func=ACT.Gelu,
-                    bias=vec_cols[:, row : row + 1],
-                )
-            hid_ps = psum.tile([P, CHUNK], F32, tag="bank", name="hid_ps%d" % c)
-            for s in range(SLICES):
-                nc.tensor.transpose(hid_ps[:, s * P : (s + 1) * P], geluT[:, s, :], ident_f32[:])
+        def multiply(c):
+            nc.tensor.matmul_mx(
+                out=hid_ps[c][:],
+                lhsT=h2_codes[:].bitcast(FP8X4),
+                lhsT_scale=h2_scales[:],
+                rhs=w1_codes[:, c, :].bitcast(FP8X4),
+                rhs_scale=w1_scales[:, c, :],
+                start=True,
+                stop=True,
+            )
+
+        def finish(c):
+            feats = slice(c * CHUNK, (c + 1) * CHUNK)
+            pre = keep.tile([P, CHUNK], F32, name="pre%d" % c)
+            nc.vector.tensor_tensor(out=pre[:], in0=hid_ps[c][:], in1=b1_all[:, feats], op=ALU.add)
             hid_sb = keep.tile([P, CHUNK], F32, name="hid_sb%d" % c)
-            nc.vector.tensor_copy(out=hid_sb[:], in_=hid_ps[:])
-            nc.sync.dma_start(out=hid_rows[:, c * CHUNK : (c + 1) * CHUNK], in_=hid_sb[:])
+            nc.scalar.activation(out=hid_sb[:], in_=pre[:], func=ACT.Gelu)
+            nc.sync.dma_start(out=hid_rows[:, feats], in_=hid_sb[:])
+
+        multiply(0)
+        multiply(1)
+        regroup_on_vector(nc, w1_grp[2], w1_raw[2], VECTOR_COLS_W1)
+        finish(0)
+        quantise_w1(2)
+        multiply(2)
+        regroup_on_vector(nc, w1_grp[3], w1_raw[3], VECTOR_COLS_W1)
+        finish(1)
+        quantise_w1(3)
+        multiply(3)
+        finish(2)
+        finish(3)

@@ -23,7 +23,7 @@ CHUNK = 512
 CHUNKS_2 = F // CHUNK
 RUN = 4
 VECTOR_COLS_WO = 384
-VECTOR_COLS_W1 = 256
+VECTOR_COLS_W1 = 192
 G_ROW = 0
 B_ROW = D // P
 B1_ROW = 2 * (D // P)
@@ -68,10 +68,6 @@ def tile_transformerblock_pb_s_kernel(
         psum = ctx.enter_context(tc.psum_pool(name="psum", bufs=8))
         ctx.enter_context(tc.manual_schedule())
 
-        ident_bf16 = keep.tile([P, P], BF16, name="ident_bf16")
-        make_identity(nc, ident_bf16[:])
-        ident_f32 = keep.tile([P, P], F32, name="ident_f32")
-        make_identity(nc, ident_f32[:])
         bias_rows = keep.tile([P, D], BF16, name="bias_rows")
         nc.vector.memset(bias_rows[:], 0.0)
         vec_rows = keep.tile([P, P], BF16, name="vec_rows")
@@ -82,10 +78,22 @@ def tile_transformerblock_pb_s_kernel(
         nc.vector.memset(neg_half[:], -0.5)
         warm = keep.tile([P, 1], F32, name="warm")
         nc.vector.memset(warm[:], 0.0)
+        ident_f32 = keep.tile([P, P], F32, name="ident_f32")
+        make_identity(nc, ident_f32[:])
+        nc.gpsimd.dma_start(out=bias_rows[0:1, :], in_=b_out.rearrange("(o d) -> o d", o=1))
+        ident_bf16 = keep.tile([P, P], BF16, name="ident_bf16")
+        make_identity(nc, ident_bf16[:])
+        nc.gpsimd.dma_start(
+            out=vec_rows[B1_ROW:VEC_ROWS, :], in_=b1.rearrange("(r c) -> r c", c=P)
+        )
+        nc.gpsimd.dma_start(
+            out=vec_rows[G_ROW:B_ROW, :], in_=ln2_g.rearrange("(r c) -> r c", c=P)
+        )
+        nc.gpsimd.dma_start(
+            out=vec_rows[B_ROW:B1_ROW, :], in_=ln2_b.rearrange("(r c) -> r c", c=P)
+        )
 
         x_sb = keep.tile([P, D], BF16, name="x_sb")
-        nc.scalar.dma_start(out=x_sb[:], in_=x.rearrange("b t d -> (b t) d"))
-        nc.scalar.dma_start(out=bias_rows[0:1, :], in_=b_out.rearrange("(o d) -> o d", o=1))
         attn_sb = keep.tile([P, A], BF16, name="attn_sb")
         wo_raw = [keep.tile([P, PACK, D], BF16, name="wo_raw%d" % g) for g in range(PASSES_1)]
 
@@ -100,15 +108,7 @@ def tile_transformerblock_pb_s_kernel(
         load_w_out(0)
         nc.sync.dma_start(out=attn_sb[:], in_=attn.rearrange("b t a -> (b t) a"))
         load_w_out(1)
-        nc.scalar.dma_start(
-            out=vec_rows[B1_ROW:VEC_ROWS, :], in_=b1.rearrange("(r c) -> r c", c=P)
-        )
-        nc.scalar.dma_start(
-            out=vec_rows[G_ROW:B_ROW, :], in_=ln2_g.rearrange("(r c) -> r c", c=P)
-        )
-        nc.scalar.dma_start(
-            out=vec_rows[B_ROW:B1_ROW, :], in_=ln2_b.rearrange("(r c) -> r c", c=P)
-        )
+        nc.sync.dma_start(out=x_sb[:], in_=x.rearrange("b t d -> (b t) d"))
         w1_raw = [keep.tile([P, PACK, CHUNK], BF16, name="w1_raw%d" % c) for c in range(CHUNKS_2)]
         for c in range(CHUNKS_2):
             nc.sync.dma_start(
@@ -138,10 +138,6 @@ def tile_transformerblock_pb_s_kernel(
         def quantise_w1(c):
             quantise(nc, w1_codes[:, c, :], w1_scales[:, c, :], w1_grp[c][:])
 
-        xb_ps = psum.tile([P, D], F32, tag="bank", name="xb_ps")
-        nc.tensor.matmul(xb_ps[:], lhsT=ident_bf16[:], rhs=x_sb[:], start=True, stop=False)
-        nc.tensor.matmul(xb_ps[:], lhsT=ones_bf16[:], rhs=bias_rows[:], start=False, stop=True)
-
         regroup_on_vector(nc, wo_grp[0], wo_raw[0], VECTOR_COLS_WO)
         regroup_on_scalar(nc, wo_grp[0], wo_raw[0], VECTOR_COLS_WO)
 
@@ -163,32 +159,16 @@ def tile_transformerblock_pb_s_kernel(
         )
         quantise_w_out(0)
 
-        vecT_ps = psum.tile([P, P], BF16, tag="bank", name="vecT_ps")
-        nc.tensor.transpose(vecT_ps[:], vec_rows[:], ident_bf16[:])
-        b1_cols = keep.tile([P, F // P], BF16, name="b1_cols")
-        nc.vector.tensor_copy(out=b1_cols[:], in_=vecT_ps[:, B1_ROW:VEC_ROWS])
-        ln_cols = keep.tile([P, B1_ROW], F32, name="ln_cols")
-        nc.vector.tensor_copy(out=ln_cols[:], in_=vecT_ps[:, 0:B1_ROW])
-
-        b1_all = keep.tile([P, F], BF16, name="b1_all")
-        b1_ps = [
-            psum.tile([P, BANK_BF16], BF16, tag="bank", name="b1_ps%d" % half)
-            for half in range(F // BANK_BF16)
-        ]
-        for r in range(F // P):
-            first = (r * P) % BANK_BF16
-            nc.tensor.transpose(
-                b1_ps[r * P // BANK_BF16][:, first : first + P],
-                b1_cols[:, r : r + 1].to_broadcast([P, P]),
-                ident_bf16[:],
-            )
-
         regroup_on_vector(nc, wo_grp[1], wo_raw[1], VECTOR_COLS_WO)
         regroup_on_scalar(nc, wo_grp[1], wo_raw[1], VECTOR_COLS_WO)
         attn_codes = keep.tile([P, PASSES_1 * P], U32, name="attn_codes", align_bytes=64)
         attn_scales = keep.tile([P, PASSES_1 * P], U8, name="attn_scales", align_bytes=64)
         quantise(nc, attn_codes[:], attn_scales[:], attn_grp[:])
         quantise_w_out(1)
+
+        xb_ps = psum.tile([P, D], F32, tag="bank", name="xb_ps")
+        nc.tensor.matmul(xb_ps[:], lhsT=ident_bf16[:], rhs=x_sb[:], start=True, stop=False)
+        nc.tensor.matmul(xb_ps[:], lhsT=ones_bf16[:], rhs=bias_rows[:], start=False, stop=True)
         xb_sb = keep.tile([P, D], F32, name="xb_sb")
         nc.scalar.copy(out=xb_sb[:], in_=xb_ps[:])
 
@@ -206,16 +186,38 @@ def tile_transformerblock_pb_s_kernel(
             )
         regroup_on_vector(nc, w1_grp[0], w1_raw[0], VECTOR_COLS_W1)
         regroup_on_scalar(nc, w1_grp[0], w1_raw[0], VECTOR_COLS_W1)
-        for half in range(F // BANK_BF16):
-            nc.scalar.copy(
-                out=b1_all[:, half * BANK_BF16 : (half + 1) * BANK_BF16], in_=b1_ps[half][:]
-            )
-        regroup_on_scalar(nc, w1_grp[1], w1_raw[1], VECTOR_COLS_W1)
-        regroup_on_scalar(nc, w1_grp[2], w1_raw[2], VECTOR_COLS_W1)
-
         x_mid = keep.tile([P, D], F32, name="x_mid")
         nc.vector.tensor_tensor(out=x_mid[:], in0=acc1_ps[:], in1=xb_sb[:], op=ALU.add)
         nc.sync.dma_start(out=out_0.rearrange("b t d -> (b t) d"), in_=x_mid[:])
+
+        vecT_ps = psum.tile([P, P], BF16, tag="bank", name="vecT_ps")
+        nc.tensor.transpose(vecT_ps[:], vec_rows[:], ident_bf16[:])
+        b1_cols = keep.tile([P, F // P], BF16, name="b1_cols")
+        nc.scalar.copy(out=b1_cols[:], in_=vecT_ps[:, B1_ROW:VEC_ROWS])
+        ln_cols = keep.tile([P, B1_ROW], F32, name="ln_cols")
+        nc.scalar.copy(out=ln_cols[:], in_=vecT_ps[:, 0:B1_ROW])
+        regroup_on_scalar(nc, w1_grp[1], w1_raw[1], VECTOR_COLS_W1)
+        regroup_on_scalar(nc, w1_grp[2], w1_raw[2], VECTOR_COLS_W1)
+
+        b1_all = keep.tile([P, F], BF16, name="b1_all")
+        b1_ps = [
+            psum.tile([P, BANK_BF16], BF16, tag="bank", name="b1_ps%d" % half)
+            for half in range(F // BANK_BF16)
+        ]
+        for r in range(F // P):
+            first = (r * P) % BANK_BF16
+            nc.tensor.transpose(
+                b1_ps[r * P // BANK_BF16][:, first : first + P],
+                b1_cols[:, r : r + 1].to_broadcast([P, P]),
+                ident_bf16[:],
+            )
+
+        def copy_b1(half):
+            nc.scalar.copy(
+                out=b1_all[:, half * BANK_BF16 : (half + 1) * BANK_BF16], in_=b1_ps[half][:]
+            )
+
+        copy_b1(0)
 
         stats = keep.tile([P, 6], F32, name="stats")
         nc.vector.bn_stats(out=stats[:], in_=x_mid[:])
@@ -226,6 +228,7 @@ def tile_transformerblock_pb_s_kernel(
         rstd = keep.tile([P, 1], F32, name="rstd")
         nc.gpsimd.tensor_tensor(out=rstd[:], in0=var_eps[:], in1=neg_half[:], op=ALU.pow)
         quantise_w1(0)
+        regroup_on_vector(nc, w1_grp[1], w1_raw[1], VECTOR_COLS_W1)
         z = keep.tile([P, D], F32, name="z")
         nc.vector.tensor_scalar(
             out=z[:],
@@ -244,7 +247,7 @@ def tile_transformerblock_pb_s_kernel(
             nc.tensor.transpose(
                 zT_ps[t // 2][:, t % 2, :], z[:, t * P : (t + 1) * P], ident_f32[:]
             )
-        regroup_on_vector(nc, w1_grp[1], w1_raw[1], VECTOR_COLS_W1)
+        quantise_w1(1)
         h2_planes = keep.tile([P, PACK, P], BF16, name="h2_planes")
         for t in range(PACK):
             gain = ln_cols[:, G_ROW + t : G_ROW + t + 1]
@@ -267,9 +270,10 @@ def tile_transformerblock_pb_s_kernel(
                     bias=bias,
                 )
         regroup_on_scalar(nc, w1_grp[3], w1_raw[3], VECTOR_COLS_W1)
+        copy_b1(1)
         h2_grp = keep.tile([P, P, PACK], BF16, name="h2_grp", align_bytes=64)
         regroup_on_vector(nc, h2_grp, h2_planes, P)
-        quantise_w1(1)
+        regroup_on_vector(nc, w1_grp[2], w1_raw[2], VECTOR_COLS_W1)
         h2_codes = keep.tile([P, P], U32, name="h2_codes", align_bytes=64)
         h2_scales = keep.tile([P, P], U8, name="h2_scales", align_bytes=64)
         quantise(nc, h2_codes[:], h2_scales[:], h2_grp[:])
@@ -300,10 +304,9 @@ def tile_transformerblock_pb_s_kernel(
 
         multiply(0)
         multiply(1)
-        regroup_on_vector(nc, w1_grp[2], w1_raw[2], VECTOR_COLS_W1)
-        finish(0)
         quantise_w1(2)
         multiply(2)
+        finish(0)
         regroup_on_vector(nc, w1_grp[3], w1_raw[3], VECTOR_COLS_W1)
         finish(1)
         quantise_w1(3)

@@ -22,7 +22,7 @@ PASSES_1 = A // K_PASS
 CHUNK = 512
 CHUNKS_2 = F // CHUNK
 RUN = 4
-VECTOR_COLS_WO = 384
+VECTOR_COLS_WO = 320
 VECTOR_COLS_W1 = 192
 G_ROW = 0
 B_ROW = D // P
@@ -294,22 +294,25 @@ def tile_transformerblock_pb_s_kernel(
                 stop=True,
             )
 
-        def finish(c):
-            feats = slice(c * CHUNK, (c + 1) * CHUNK)
-            pre = keep.tile([P, CHUNK], F32, name="pre%d" % c)
-            nc.vector.tensor_tensor(out=pre[:], in0=hid_ps[c][:], in1=b1_all[:, feats], op=ALU.add)
-            hid_sb = keep.tile([P, CHUNK], F32, name="hid_sb%d" % c)
+        def finish(first, width):
+            feats = slice(first, first + width)
+            in_bank = slice(first % CHUNK, first % CHUNK + width)
+            pre = keep.tile([P, width], F32, name="pre%d" % first)
+            nc.vector.tensor_tensor(
+                out=pre[:], in0=hid_ps[first // CHUNK][:, in_bank], in1=b1_all[:, feats], op=ALU.add
+            )
+            hid_sb = keep.tile([P, width], F32, name="hid_sb%d" % first)
             nc.scalar.activation(out=hid_sb[:], in_=pre[:], func=ACT.Gelu)
             nc.sync.dma_start(out=hid_rows[:, feats], in_=hid_sb[:])
 
         multiply(0)
         multiply(1)
+        regroup_on_vector(nc, w1_grp[3], w1_raw[3], VECTOR_COLS_W1)
         quantise_w1(2)
         multiply(2)
-        finish(0)
-        regroup_on_vector(nc, w1_grp[3], w1_raw[3], VECTOR_COLS_W1)
-        finish(1)
         quantise_w1(3)
         multiply(3)
-        finish(2)
-        finish(3)
+        for c in range(CHUNKS_2 - 1):
+            finish(c * CHUNK, CHUNK)
+        for half in range(2):
+            finish((CHUNKS_2 - 1) * CHUNK + half * (CHUNK // 2), CHUNK // 2)

@@ -23,7 +23,7 @@ CHUNK = 512
 CHUNKS_2 = F // CHUNK
 RUN = 4
 VECTOR_COLS_WO = 320
-VECTOR_COLS_W1 = 192
+VECTOR_COLS_W1 = 128
 G_ROW = 0
 B_ROW = D // P
 B1_ROW = 2 * (D // P)

@@ -80,16 +80,16 @@ def tile_transformerblock_pb_s_kernel(
         nc.vector.memset(warm[:], 0.0)
         ident_f32 = keep.tile([P, P], F32, name="ident_f32")
         make_identity(nc, ident_f32[:])
-        nc.gpsimd.dma_start(out=bias_rows[0:1, :], in_=b_out.rearrange("(o d) -> o d", o=1))
         ident_bf16 = keep.tile([P, P], BF16, name="ident_bf16")
         make_identity(nc, ident_bf16[:])
-        nc.gpsimd.dma_start(
+        nc.scalar.dma_start(out=bias_rows[0:1, :], in_=b_out.rearrange("(o d) -> o d", o=1))
+        nc.scalar.dma_start(
             out=vec_rows[B1_ROW:VEC_ROWS, :], in_=b1.rearrange("(r c) -> r c", c=P)
         )
-        nc.gpsimd.dma_start(
+        nc.scalar.dma_start(
             out=vec_rows[G_ROW:B_ROW, :], in_=ln2_g.rearrange("(r c) -> r c", c=P)
         )
-        nc.gpsimd.dma_start(
+        nc.scalar.dma_start(
             out=vec_rows[B_ROW:B1_ROW, :], in_=ln2_b.rearrange("(r c) -> r c", c=P)
         )
 

@@ -24,11 +24,11 @@ CHUNKS_2 = F // CHUNK
 RUN = 4
 VECTOR_COLS_WO = 320
 VECTOR_COLS_W1 = 128
-G_ROW = 0
-B_ROW = D // P
-B1_ROW = 2 * (D // P)
-VEC_ROWS = B1_ROW + F // P
-BANK_BF16 = 1024
+D_ROWS = D // P
+B_ROW = P - D_ROWS
+G_ROW = B_ROW - D_ROWS
+BIAS_ROW = P - 1
+QUAD3 = 96
 
 FLOPS = 2 * P * A * D + 2 * P * D * F
 
@@ -69,9 +69,16 @@ def tile_transformerblock_pb_s_kernel(
         ctx.enter_context(tc.manual_schedule())
 
         bias_rows = keep.tile([P, D], BF16, name="bias_rows")
-        nc.vector.memset(bias_rows[:], 0.0)
         vec_rows = keep.tile([P, P], BF16, name="vec_rows")
-        nc.vector.memset(vec_rows[:], 0.0)
+        nc.scalar.dma_start(
+            out=bias_rows[BIAS_ROW : BIAS_ROW + 1, :], in_=b_out.rearrange("(o d) -> o d", o=1)
+        )
+        nc.scalar.dma_start(out=vec_rows[G_ROW:B_ROW, :], in_=ln2_g.rearrange("(r c) -> r c", c=P))
+        nc.scalar.dma_start(out=vec_rows[B_ROW:P, :], in_=ln2_b.rearrange("(r c) -> r c", c=P))
+        for rows, end in ((vec_rows, G_ROW), (bias_rows, BIAS_ROW)):
+            zeros = rows[:].bitcast(U32)
+            nc.vector.memset(zeros[0:QUAD3, :], 0)
+            nc.vector.memset(zeros[QUAD3:end, :], 0)
         ones_bf16 = keep.tile([P, P], BF16, name="ones_bf16")
         nc.vector.memset(ones_bf16[:], 1.0)
         neg_half = keep.tile([P, 1], F32, name="neg_half")
@@ -82,16 +89,6 @@ def tile_transformerblock_pb_s_kernel(
         make_identity(nc, ident_f32[:])
         ident_bf16 = keep.tile([P, P], BF16, name="ident_bf16")
         make_identity(nc, ident_bf16[:])
-        nc.scalar.dma_start(out=bias_rows[0:1, :], in_=b_out.rearrange("(o d) -> o d", o=1))
-        nc.scalar.dma_start(
-            out=vec_rows[B1_ROW:VEC_ROWS, :], in_=b1.rearrange("(r c) -> r c", c=P)
-        )
-        nc.scalar.dma_start(
-            out=vec_rows[G_ROW:B_ROW, :], in_=ln2_g.rearrange("(r c) -> r c", c=P)
-        )
-        nc.scalar.dma_start(
-            out=vec_rows[B_ROW:B1_ROW, :], in_=ln2_b.rearrange("(r c) -> r c", c=P)
-        )
 
         x_sb = keep.tile([P, D], BF16, name="x_sb")
         attn_sb = keep.tile([P, A], BF16, name="attn_sb")
@@ -99,10 +96,8 @@ def tile_transformerblock_pb_s_kernel(
 
         def load_w_out(g):
             nc.sync.dma_start(
-                out=wo_raw[g][:].rearrange("q (u e) c -> q u (e c)", e=2),
-                in_=w_out[g * K_PASS : (g + 1) * K_PASS, :].rearrange(
-                    "(u q e) c -> q u (e c)", u=2, e=2
-                ),
+                out=wo_raw[g][:],
+                in_=w_out[g * K_PASS : (g + 1) * K_PASS, :].rearrange("(p t) c -> p t c", t=PACK),
             )
 
         load_w_out(0)
@@ -113,8 +108,11 @@ def tile_transformerblock_pb_s_kernel(
         for c in range(CHUNKS_2):
             nc.sync.dma_start(
                 out=w1_raw[c][:],
-                in_=w1[:, c * CHUNK : (c + 1) * CHUNK].rearrange("(t p) n -> p t n", p=P),
+                in_=w1[:, c * CHUNK : (c + 1) * CHUNK].rearrange("(p t) n -> p t n", t=PACK),
             )
+
+        b1_all = keep.tile([P, F], BF16, name="b1_all")
+        nc.sync.dma_start(out=b1_all[:], in_=b1.partition_broadcast(P))
 
         warm_out = keep.tile([P, 1], F32, name="warm_out")
         nc.scalar.activation(out=warm_out[:], in_=warm[:], func=ACT.Gelu)
@@ -145,10 +143,8 @@ def tile_transformerblock_pb_s_kernel(
         attnT_ps = psum.tile([P, PASSES_1, 2, P], F32, tag="bank", name="attnT_ps")
         for g in range(PASSES_1):
             for u in range(2):
-                first = (2 * g + u) * P
-                nc.tensor.transpose(
-                    attnT_ps[:, g, u, :], attn_words[:, first : first + P], ident_f32[:]
-                )
+                words = slice(2 * P * g + u, 2 * P * (g + 1), 2)
+                nc.tensor.transpose(attnT_ps[:, g, u, :], attn_words[:, words], ident_f32[:])
         attn_grp = keep.tile([P, PASSES_1 * P, PACK], BF16, name="attn_grp", align_bytes=64)
         nc.scalar.copy(
             out=attn_grp[:]
@@ -165,6 +161,11 @@ def tile_transformerblock_pb_s_kernel(
         attn_scales = keep.tile([P, PASSES_1 * P], U8, name="attn_scales", align_bytes=64)
         quantise(nc, attn_codes[:], attn_scales[:], attn_grp[:])
         quantise_w_out(1)
+
+        vecT_ps = psum.tile([P, P], BF16, tag="bank", name="vecT_ps")
+        nc.tensor.transpose(vecT_ps[:], vec_rows[:], ident_bf16[:])
+        ln_cols = keep.tile([P, 2 * D_ROWS], BF16, name="ln_cols")
+        nc.scalar.copy(out=ln_cols[:], in_=vecT_ps[:, G_ROW:P])
 
         xb_ps = psum.tile([P, D], F32, tag="bank", name="xb_ps")
         nc.tensor.matmul(xb_ps[:], lhsT=ident_bf16[:], rhs=x_sb[:], start=True, stop=False)
@@ -187,93 +188,70 @@ def tile_transformerblock_pb_s_kernel(
         regroup_on_vector(nc, w1_grp[0], w1_raw[0], VECTOR_COLS_W1)
         regroup_on_scalar(nc, w1_grp[0], w1_raw[0], VECTOR_COLS_W1)
         x_mid = keep.tile([P, D], F32, name="x_mid")
-        nc.vector.tensor_tensor(out=x_mid[:], in0=acc1_ps[:], in1=xb_sb[:], op=ALU.add)
+        halves = [slice(h * (D // 2), (h + 1) * (D // 2)) for h in range(2)]
+        for half in halves:
+            nc.vector.tensor_tensor(
+                out=x_mid[:, half], in0=acc1_ps[:, half], in1=xb_sb[:, half], op=ALU.add
+            )
         nc.sync.dma_start(out=out_0.rearrange("b t d -> (b t) d"), in_=x_mid[:])
 
-        vecT_ps = psum.tile([P, P], BF16, tag="bank", name="vecT_ps")
-        nc.tensor.transpose(vecT_ps[:], vec_rows[:], ident_bf16[:])
-        b1_cols = keep.tile([P, F // P], BF16, name="b1_cols")
-        nc.scalar.copy(out=b1_cols[:], in_=vecT_ps[:, B1_ROW:VEC_ROWS])
-        ln_cols = keep.tile([P, B1_ROW], F32, name="ln_cols")
-        nc.scalar.copy(out=ln_cols[:], in_=vecT_ps[:, 0:B1_ROW])
+        ln_ps = psum.tile([P, 2, D], BF16, tag="bank", name="ln_ps")
+        for r in range(2 * D_ROWS):
+            first = (r % D_ROWS) * P
+            nc.tensor.transpose(
+                ln_ps[:, r // D_ROWS, first : first + P],
+                ln_cols[:, r : r + 1].to_broadcast([P, P]),
+                ident_bf16[:],
+            )
         regroup_on_scalar(nc, w1_grp[1], w1_raw[1], VECTOR_COLS_W1)
         regroup_on_scalar(nc, w1_grp[2], w1_raw[2], VECTOR_COLS_W1)
 
-        b1_all = keep.tile([P, F], BF16, name="b1_all")
-        b1_ps = [
-            psum.tile([P, BANK_BF16], BF16, tag="bank", name="b1_ps%d" % half)
-            for half in range(F // BANK_BF16)
-        ]
-        for r in range(F // P):
-            first = (r * P) % BANK_BF16
-            nc.tensor.transpose(
-                b1_ps[r * P // BANK_BF16][:, first : first + P],
-                b1_cols[:, r : r + 1].to_broadcast([P, P]),
-                ident_bf16[:],
-            )
-
-        def copy_b1(half):
-            nc.scalar.copy(
-                out=b1_all[:, half * BANK_BF16 : (half + 1) * BANK_BF16], in_=b1_ps[half][:]
-            )
-
-        copy_b1(0)
-
-        stats = keep.tile([P, 6], F32, name="stats")
-        nc.vector.bn_stats(out=stats[:], in_=x_mid[:])
+        stats = keep.tile([P, 2, 6], F32, name="stats")
+        for h, half in enumerate(halves):
+            nc.vector.bn_stats(out=stats[:, h, :], in_=x_mid[:, half])
+        regroup_on_vector(nc, w1_grp[1], w1_raw[1], VECTOR_COLS_W1)
         mean_var = keep.tile([P, 2], F32, name="mean_var")
         nc.vector.bn_aggr(out=mean_var[:], in_=stats[:])
         var_eps = keep.tile([P, 1], F32, name="var_eps")
         nc.vector.tensor_scalar_add(out=var_eps[:], in0=mean_var[:, 1:2], scalar1=EPS)
         rstd = keep.tile([P, 1], F32, name="rstd")
         nc.gpsimd.tensor_tensor(out=rstd[:], in0=var_eps[:], in1=neg_half[:], op=ALU.pow)
-        quantise_w1(0)
-        regroup_on_vector(nc, w1_grp[1], w1_raw[1], VECTOR_COLS_W1)
-        z = keep.tile([P, D], F32, name="z")
-        nc.vector.tensor_scalar(
-            out=z[:],
+        centred = keep.tile([P, D], F32, name="centred")
+        nc.vector.scalar_tensor_tensor(
+            out=centred[:],
             in0=x_mid[:],
-            scalar1=mean_var[:, 0:1],
-            scalar2=rstd[:],
+            scalar=mean_var[:, 0:1],
+            in1=ln_ps[:, 0, :],
             op0=ALU.subtract,
             op1=ALU.mult,
         )
+        quantise_w1(0)
 
-        zT_ps = [
-            psum.tile([P, PACK // 2, P], F32, tag="bank", name="zT_ps%d" % half)
-            for half in range(2)
-        ]
-        for t in range(PACK):
-            nc.tensor.transpose(
-                zT_ps[t // 2][:, t % 2, :], z[:, t * P : (t + 1) * P], ident_f32[:]
-            )
-        quantise_w1(1)
-        h2_planes = keep.tile([P, PACK, P], BF16, name="h2_planes")
-        for t in range(PACK):
-            gain = ln_cols[:, G_ROW + t : G_ROW + t + 1]
-            bias = ln_cols[:, B_ROW + t : B_ROW + t + 1]
-            if t // 2 == 0:
-                nc.vector.tensor_scalar(
-                    out=h2_planes[:, t, :],
-                    in0=zT_ps[0][:, t % 2, :],
-                    scalar1=gain,
-                    scalar2=bias,
-                    op0=ALU.mult,
-                    op1=ALU.add,
-                )
-            else:
-                nc.scalar.activation(
-                    out=h2_planes[:, t, :],
-                    in_=zT_ps[1][:, t % 2, :],
-                    func=ACT.Identity,
-                    scale=gain,
-                    bias=bias,
-                )
-        regroup_on_scalar(nc, w1_grp[3], w1_raw[3], VECTOR_COLS_W1)
-        copy_b1(1)
-        h2_grp = keep.tile([P, P, PACK], BF16, name="h2_grp", align_bytes=64)
-        regroup_on_vector(nc, h2_grp, h2_planes, P)
+        h2 = keep.tile([P, D], BF16, name="h2")
+        nc.vector.scalar_tensor_tensor(
+            out=h2[:],
+            in0=centred[:],
+            scalar=rstd[:],
+            in1=ln_ps[:, 1, :],
+            op0=ALU.mult,
+            op1=ALU.add,
+        )
+        h2_words = h2[:].bitcast(F32)
+        h2T_ps = psum.tile([P, 2, P], F32, tag="bank", name="h2T_ps")
+        for u in range(2):
+            nc.tensor.transpose(h2T_ps[:, u, :], h2_words[:, slice(u, 2 * P, 2)], ident_f32[:])
         regroup_on_vector(nc, w1_grp[2], w1_raw[2], VECTOR_COLS_W1)
+        quantise_w1(1)
+        h2_grp = keep.tile([P, P, PACK], BF16, name="h2_grp", align_bytes=64)
+        nc.vector.tensor_copy(
+            out=h2_grp[:]
+            .rearrange("p r t -> p (r t)")
+            .bitcast(F32)
+            .rearrange("p (r u) -> p r u", u=2),
+            in_=h2T_ps[:].rearrange("p u r -> p r u"),
+        )
+        regroup_on_scalar(nc, w1_grp[3], w1_raw[3], VECTOR_COLS_W1)
+        regroup_on_vector(nc, w1_grp[3], w1_raw[3], VECTOR_COLS_W1)
         h2_codes = keep.tile([P, P], U32, name="h2_codes", align_bytes=64)
         h2_scales = keep.tile([P, P], U8, name="h2_scales", align_bytes=64)
         quantise(nc, h2_codes[:], h2_scales[:], h2_grp[:])
@@ -305,14 +283,17 @@ def tile_transformerblock_pb_s_kernel(
             nc.scalar.activation(out=hid_sb[:], in_=pre[:], func=ACT.Gelu)
             nc.sync.dma_start(out=hid_rows[:, feats], in_=hid_sb[:])
 
+        def finish_in_halves(c):
+            for half in range(2):
+                finish(c * CHUNK + half * (CHUNK // 2), CHUNK // 2)
+
         multiply(0)
         multiply(1)
-        regroup_on_vector(nc, w1_grp[3], w1_raw[3], VECTOR_COLS_W1)
         quantise_w1(2)
         multiply(2)
+        finish_in_halves(0)
         quantise_w1(3)
         multiply(3)
-        for c in range(CHUNKS_2 - 1):
+        for c in range(1, CHUNKS_2 - 1):
             finish(c * CHUNK, CHUNK)
-        for half in range(2):
-            finish((CHUNKS_2 - 1) * CHUNK + half * (CHUNK // 2), CHUNK // 2)
+        finish_in_halves(CHUNKS_2 - 1)

@@ -22,8 +22,8 @@ PASSES_1 = A // K_PASS
 CHUNK = 512
 CHUNKS_2 = F // CHUNK
 RUN = 4
-VECTOR_COLS_WO = 320
-VECTOR_COLS_W1 = 128
+VECTOR_COLS_WO = (320, 384)
+VECTOR_COLS_W1 = (128, 64, 64, 64)
 D_ROWS = D // P
 B_ROW = P - D_ROWS
 G_ROW = B_ROW - D_ROWS
@@ -43,6 +43,17 @@ def regroup_on_vector(nc, grouped, raw, vector_cols):
     dst, src = regroup_views(grouped, raw)
     split = vector_cols // RUN
     nc.vector.tensor_copy(out=dst[:, :split], in_=src[:, :split])
+
+
+def regroup_on_gpsimd(nc, grouped, raw, vector_cols, one):
+    nc.gpsimd.tensor_scalar(
+        out=grouped[:, vector_cols:, :],
+        in0=raw[:, :, vector_cols:].rearrange("p t c -> p c t"),
+        scalar1=one,
+        scalar2=0.0,
+        op0=ALU.mult,
+        op1=ALU.add,
+    )
 
 
 def regroup_on_scalar(nc, grouped, raw, vector_cols):
@@ -136,8 +147,8 @@ def tile_transformerblock_pb_s_kernel(
         def quantise_w1(c):
             quantise(nc, w1_codes[:, c, :], w1_scales[:, c, :], w1_grp[c][:])
 
-        regroup_on_vector(nc, wo_grp[0], wo_raw[0], VECTOR_COLS_WO)
-        regroup_on_scalar(nc, wo_grp[0], wo_raw[0], VECTOR_COLS_WO)
+        regroup_on_vector(nc, wo_grp[0], wo_raw[0], VECTOR_COLS_WO[0])
+        regroup_on_scalar(nc, wo_grp[0], wo_raw[0], VECTOR_COLS_WO[0])
 
         attn_words = attn_sb[:].bitcast(F32)
         attnT_ps = psum.tile([P, PASSES_1, 2, P], F32, tag="bank", name="attnT_ps")
@@ -155,8 +166,8 @@ def tile_transformerblock_pb_s_kernel(
         )
         quantise_w_out(0)
 
-        regroup_on_vector(nc, wo_grp[1], wo_raw[1], VECTOR_COLS_WO)
-        regroup_on_scalar(nc, wo_grp[1], wo_raw[1], VECTOR_COLS_WO)
+        regroup_on_vector(nc, wo_grp[1], wo_raw[1], VECTOR_COLS_WO[1])
+        regroup_on_scalar(nc, wo_grp[1], wo_raw[1], VECTOR_COLS_WO[1])
         attn_codes = keep.tile([P, PASSES_1 * P], U32, name="attn_codes", align_bytes=64)
         attn_scales = keep.tile([P, PASSES_1 * P], U8, name="attn_scales", align_bytes=64)
         quantise(nc, attn_codes[:], attn_scales[:], attn_grp[:])
@@ -168,30 +179,34 @@ def tile_transformerblock_pb_s_kernel(
         nc.scalar.copy(out=ln_cols[:], in_=vecT_ps[:, G_ROW:P])
 
         xb_ps = psum.tile([P, D], F32, tag="bank", name="xb_ps")
-        nc.tensor.matmul(xb_ps[:], lhsT=ident_bf16[:], rhs=x_sb[:], start=True, stop=False)
-        nc.tensor.matmul(xb_ps[:], lhsT=ones_bf16[:], rhs=bias_rows[:], start=False, stop=True)
+        nc.tensor.matmul(xb_ps[:], lhsT=ones_bf16[:], rhs=bias_rows[:], start=True, stop=False)
+        nc.tensor.matmul(xb_ps[:], lhsT=ident_bf16[:], rhs=x_sb[:], start=False, stop=True)
         xb_sb = keep.tile([P, D], F32, name="xb_sb")
         nc.scalar.copy(out=xb_sb[:], in_=xb_ps[:])
 
-        acc1_ps = psum.tile([P, D], F32, tag="bank", name="acc1_ps")
+        halves = [slice(h * (D // 2), (h + 1) * (D // 2)) for h in range(2)]
+        acc1_ps = [psum.tile([P, D // 2], F32, tag="bank", name="acc1_ps%d" % h) for h in range(2)]
         for g in range(PASSES_1):
             tokens = slice(g * P, (g + 1) * P)
-            nc.tensor.matmul_mx(
-                out=acc1_ps[:],
-                lhsT=attn_codes[:, tokens].bitcast(FP8X4),
-                lhsT_scale=attn_scales[:, tokens],
-                rhs=wo_codes[:, g, :].bitcast(FP8X4),
-                rhs_scale=wo_scales[:, g, :],
-                start=(g == 0),
-                stop=(g == PASSES_1 - 1),
-            )
-        regroup_on_vector(nc, w1_grp[0], w1_raw[0], VECTOR_COLS_W1)
-        regroup_on_scalar(nc, w1_grp[0], w1_raw[0], VECTOR_COLS_W1)
+            for h, half in enumerate(halves):
+                nc.tensor.matmul_mx(
+                    out=acc1_ps[h][:],
+                    lhsT=attn_codes[:, tokens].bitcast(FP8X4),
+                    lhsT_scale=attn_scales[:, tokens],
+                    rhs=wo_codes[:, g, half].bitcast(FP8X4),
+                    rhs_scale=wo_scales[:, g, half],
+                    start=(g == 0),
+                    stop=(g == PASSES_1 - 1),
+                )
+        regroup_on_vector(nc, w1_grp[0], w1_raw[0], VECTOR_COLS_W1[0])
+        one = keep.tile([P, 1], F32, name="one")
+        nc.vector.memset(one[:], 1.0)
+        regroup_on_gpsimd(nc, w1_grp[0], w1_raw[0], VECTOR_COLS_W1[0], one[:])
+        regroup_on_scalar(nc, w1_grp[1], w1_raw[1], VECTOR_COLS_W1[1])
         x_mid = keep.tile([P, D], F32, name="x_mid")
-        halves = [slice(h * (D // 2), (h + 1) * (D // 2)) for h in range(2)]
-        for half in halves:
+        for h, half in enumerate(halves):
             nc.vector.tensor_tensor(
-                out=x_mid[:, half], in0=acc1_ps[:, half], in1=xb_sb[:, half], op=ALU.add
+                out=x_mid[:, half], in0=acc1_ps[h][:], in1=xb_sb[:, half], op=ALU.add
             )
         nc.sync.dma_start(out=out_0.rearrange("b t d -> (b t) d"), in_=x_mid[:])
 
@@ -203,13 +218,12 @@ def tile_transformerblock_pb_s_kernel(
                 ln_cols[:, r : r + 1].to_broadcast([P, P]),
                 ident_bf16[:],
             )
-        regroup_on_scalar(nc, w1_grp[1], w1_raw[1], VECTOR_COLS_W1)
-        regroup_on_scalar(nc, w1_grp[2], w1_raw[2], VECTOR_COLS_W1)
+        regroup_on_scalar(nc, w1_grp[2], w1_raw[2], VECTOR_COLS_W1[2])
 
         stats = keep.tile([P, 2, 6], F32, name="stats")
         for h, half in enumerate(halves):
             nc.vector.bn_stats(out=stats[:, h, :], in_=x_mid[:, half])
-        regroup_on_vector(nc, w1_grp[1], w1_raw[1], VECTOR_COLS_W1)
+        regroup_on_vector(nc, w1_grp[1], w1_raw[1], VECTOR_COLS_W1[1])
         mean_var = keep.tile([P, 2], F32, name="mean_var")
         nc.vector.bn_aggr(out=mean_var[:], in_=stats[:])
         var_eps = keep.tile([P, 1], F32, name="var_eps")
@@ -240,7 +254,7 @@ def tile_transformerblock_pb_s_kernel(
         h2T_ps = psum.tile([P, 2, P], F32, tag="bank", name="h2T_ps")
         for u in range(2):
             nc.tensor.transpose(h2T_ps[:, u, :], h2_words[:, slice(u, 2 * P, 2)], ident_f32[:])
-        regroup_on_vector(nc, w1_grp[2], w1_raw[2], VECTOR_COLS_W1)
+        regroup_on_vector(nc, w1_grp[2], w1_raw[2], VECTOR_COLS_W1[2])
         quantise_w1(1)
         h2_grp = keep.tile([P, P, PACK], BF16, name="h2_grp", align_bytes=64)
         nc.vector.tensor_copy(
@@ -250,50 +264,47 @@ def tile_transformerblock_pb_s_kernel(
             .rearrange("p (r u) -> p r u", u=2),
             in_=h2T_ps[:].rearrange("p u r -> p r u"),
         )
-        regroup_on_scalar(nc, w1_grp[3], w1_raw[3], VECTOR_COLS_W1)
-        regroup_on_vector(nc, w1_grp[3], w1_raw[3], VECTOR_COLS_W1)
+        regroup_on_scalar(nc, w1_grp[3], w1_raw[3], VECTOR_COLS_W1[3])
+        regroup_on_vector(nc, w1_grp[3], w1_raw[3], VECTOR_COLS_W1[3])
         h2_codes = keep.tile([P, P], U32, name="h2_codes", align_bytes=64)
         h2_scales = keep.tile([P, P], U8, name="h2_scales", align_bytes=64)
         quantise(nc, h2_codes[:], h2_scales[:], h2_grp[:])
 
         hid_rows = out_1.rearrange("b t f -> (b t) f")
-        hid_ps = [
-            psum.tile([P, CHUNK], F32, tag="bank", name="hid_ps%d" % c) for c in range(CHUNKS_2)
-        ]
+        def multiply(c, parts):
+            width = CHUNK // parts
+            banks = []
+            for i in range(parts):
+                cols = slice(i * width, (i + 1) * width)
+                bank = psum.tile([P, width], F32, tag="bank", name="hid_ps%d_%d" % (c, i))
+                nc.tensor.matmul_mx(
+                    out=bank[:],
+                    lhsT=h2_codes[:].bitcast(FP8X4),
+                    lhsT_scale=h2_scales[:],
+                    rhs=w1_codes[:, c, cols].bitcast(FP8X4),
+                    rhs_scale=w1_scales[:, c, cols],
+                    start=True,
+                    stop=True,
+                )
+                banks.append((c * CHUNK + i * width, width, bank))
+            return banks
 
-        def multiply(c):
-            nc.tensor.matmul_mx(
-                out=hid_ps[c][:],
-                lhsT=h2_codes[:].bitcast(FP8X4),
-                lhsT_scale=h2_scales[:],
-                rhs=w1_codes[:, c, :].bitcast(FP8X4),
-                rhs_scale=w1_scales[:, c, :],
-                start=True,
-                stop=True,
-            )
-
-        def finish(first, width):
+        def finish(first, width, bank):
             feats = slice(first, first + width)
-            in_bank = slice(first % CHUNK, first % CHUNK + width)
             pre = keep.tile([P, width], F32, name="pre%d" % first)
-            nc.vector.tensor_tensor(
-                out=pre[:], in0=hid_ps[first // CHUNK][:, in_bank], in1=b1_all[:, feats], op=ALU.add
-            )
+            nc.vector.tensor_tensor(out=pre[:], in0=bank[:], in1=b1_all[:, feats], op=ALU.add)
             hid_sb = keep.tile([P, width], F32, name="hid_sb%d" % first)
             nc.scalar.activation(out=hid_sb[:], in_=pre[:], func=ACT.Gelu)
             nc.sync.dma_start(out=hid_rows[:, feats], in_=hid_sb[:])
 
-        def finish_in_halves(c):
-            for half in range(2):
-                finish(c * CHUNK + half * (CHUNK // 2), CHUNK // 2)
-
-        multiply(0)
-        multiply(1)
+        parts_of = [2, 1, 1, 2]
+        products = [multiply(c, parts_of[c]) for c in range(2)]
         quantise_w1(2)
-        multiply(2)
-        finish_in_halves(0)
+        products.append(multiply(2, parts_of[2]))
+        for part in products[0]:
+            finish(*part)
         quantise_w1(3)
-        multiply(3)
-        for c in range(1, CHUNKS_2 - 1):
-            finish(c * CHUNK, CHUNK)
-        finish_in_halves(CHUNKS_2 - 1)
+        products.append(multiply(3, parts_of[3]))
+        for product in products[1:]:
+            for part in product:
+                finish(*part)

from contextlib import ExitStack

import concourse.mybir as mybir
from concourse.masks import make_identity

BF16 = mybir.dt.bfloat16
F32 = mybir.dt.float32
U32 = mybir.dt.uint32
U8 = mybir.dt.uint8
FP8X4 = mybir.dt.float8_e4m3fn_x4
ACT = mybir.ActivationFunctionType
ALU = mybir.AluOpType

P = 128
PACK = 4
K_PASS = P * PACK
A = 1024
D = 512
F = 2048
EPS = 1e-5
PASSES_1 = A // K_PASS
CHUNK = 512
CHUNKS_2 = F // CHUNK
RUN = 4
VECTOR_COLS_WO = (320, 384)
VECTOR_COLS_W1 = (128, 64, 64, 64)
D_ROWS = D // P
B_ROW = P - D_ROWS
G_ROW = B_ROW - D_ROWS
BIAS_ROW = P - 1
QUAD3 = 96

FLOPS = 2 * P * A * D + 2 * P * D * F


def regroup_views(grouped, raw):
    src = raw[:].rearrange("p t (c i) -> p c t i", i=RUN)
    dst = grouped[:].rearrange("p (c i) t -> p c t i", i=RUN)
    return dst, src


def regroup_on_vector(nc, grouped, raw, vector_cols):
    dst, src = regroup_views(grouped, raw)
    split = vector_cols // RUN
    nc.vector.tensor_copy(out=dst[:, :split], in_=src[:, :split])


def regroup_on_gpsimd(nc, grouped, raw, vector_cols, one):
    nc.gpsimd.tensor_scalar(
        out=grouped[:, vector_cols:, :],
        in0=raw[:, :, vector_cols:].rearrange("p t c -> p c t"),
        scalar1=one,
        scalar2=0.0,
        op0=ALU.mult,
        op1=ALU.add,
    )


def regroup_on_scalar(nc, grouped, raw, vector_cols):
    dst, src = regroup_views(grouped, raw)
    split = vector_cols // RUN
    nc.scalar.copy(out=dst[:, split:], in_=src[:, split:])


def quantise(nc, codes, scales, grouped):
    nc.vector.quantize_mx(
        out=codes.bitcast(FP8X4),
        scales=scales,
        in_=grouped.rearrange("p c t -> p (c t)"),
    )


def tile_transformerblock_pb_s_kernel(
    tc, attn, x, w_out, b_out, ln2_g, ln2_b, w1, b1, out_0, out_1
):
    nc = tc.nc
    with ExitStack() as ctx:
        keep = ctx.enter_context(tc.tile_pool(name="keep", bufs=1))
        psum = ctx.enter_context(tc.psum_pool(name="psum", bufs=8))
        ctx.enter_context(tc.manual_schedule())

        bias_rows = keep.tile([P, D], BF16, name="bias_rows")
        vec_rows = keep.tile([P, P], BF16, name="vec_rows")
        nc.scalar.dma_start(
            out=bias_rows[BIAS_ROW : BIAS_ROW + 1, :], in_=b_out.rearrange("(o d) -> o d", o=1)
        )
        nc.scalar.dma_start(out=vec_rows[G_ROW:B_ROW, :], in_=ln2_g.rearrange("(r c) -> r c", c=P))
        nc.scalar.dma_start(out=vec_rows[B_ROW:P, :], in_=ln2_b.rearrange("(r c) -> r c", c=P))
        for rows, end in ((vec_rows, G_ROW), (bias_rows, BIAS_ROW)):
            zeros = rows[:].bitcast(U32)
            nc.vector.memset(zeros[0:QUAD3, :], 0)
            nc.vector.memset(zeros[QUAD3:end, :], 0)
        ones_bf16 = keep.tile([P, P], BF16, name="ones_bf16")
        nc.vector.memset(ones_bf16[:], 1.0)
        neg_half = keep.tile([P, 1], F32, name="neg_half")
        nc.vector.memset(neg_half[:], -0.5)
        warm = keep.tile([P, 1], F32, name="warm")
        nc.vector.memset(warm[:], 0.0)
        ident_f32 = keep.tile([P, P], F32, name="ident_f32")
        make_identity(nc, ident_f32[:])
        ident_bf16 = keep.tile([P, P], BF16, name="ident_bf16")
        make_identity(nc, ident_bf16[:])

        x_sb = keep.tile([P, D], BF16, name="x_sb")
        attn_sb = keep.tile([P, A], BF16, name="attn_sb")
        wo_raw = [keep.tile([P, PACK, D], BF16, name="wo_raw%d" % g) for g in range(PASSES_1)]

        def load_w_out(g):
            nc.sync.dma_start(
                out=wo_raw[g][:],
                in_=w_out[g * K_PASS : (g + 1) * K_PASS, :].rearrange("(p t) c -> p t c", t=PACK),
            )

        load_w_out(0)
        nc.sync.dma_start(out=attn_sb[:], in_=attn.rearrange("b t a -> (b t) a"))
        load_w_out(1)
        nc.sync.dma_start(out=x_sb[:], in_=x.rearrange("b t d -> (b t) d"))
        w1_raw = [keep.tile([P, PACK, CHUNK], BF16, name="w1_raw%d" % c) for c in range(CHUNKS_2)]
        for c in range(CHUNKS_2):
            nc.sync.dma_start(
                out=w1_raw[c][:],
                in_=w1[:, c * CHUNK : (c + 1) * CHUNK].rearrange("(p t) n -> p t n", t=PACK),
            )

        b1_all = keep.tile([P, F], BF16, name="b1_all")
        nc.sync.dma_start(out=b1_all[:], in_=b1.partition_broadcast(P))

        warm_out = keep.tile([P, 1], F32, name="warm_out")
        nc.scalar.activation(out=warm_out[:], in_=warm[:], func=ACT.Gelu)

        wo_grp = [
            keep.tile([P, D, PACK], BF16, name="wo_grp%d" % g, align_bytes=64)
            for g in range(PASSES_1)
        ]
        wo_codes = keep.tile([P, PASSES_1, D], U32, name="wo_codes", align_bytes=64)
        wo_scales = keep.tile([P, PASSES_1, D], U8, name="wo_scales", align_bytes=64)
        w1_grp = [
            keep.tile([P, CHUNK, PACK], BF16, name="w1_grp%d" % c, align_bytes=64)
            for c in range(CHUNKS_2)
        ]
        w1_codes = keep.tile([P, CHUNKS_2, CHUNK], U32, name="w1_codes", align_bytes=64)
        w1_scales = keep.tile([P, CHUNKS_2, CHUNK], U8, name="w1_scales", align_bytes=64)

        def quantise_w_out(g):
            quantise(nc, wo_codes[:, g, :], wo_scales[:, g, :], wo_grp[g][:])

        def quantise_w1(c):
            quantise(nc, w1_codes[:, c, :], w1_scales[:, c, :], w1_grp[c][:])

        regroup_on_vector(nc, wo_grp[0], wo_raw[0], VECTOR_COLS_WO[0])
        regroup_on_scalar(nc, wo_grp[0], wo_raw[0], VECTOR_COLS_WO[0])

        attn_words = attn_sb[:].bitcast(F32)
        attnT_ps = psum.tile([P, PASSES_1, 2, P], F32, tag="bank", name="attnT_ps")
        for g in range(PASSES_1):
            for u in range(2):
                words = slice(2 * P * g + u, 2 * P * (g + 1), 2)
                nc.tensor.transpose(attnT_ps[:, g, u, :], attn_words[:, words], ident_f32[:])
        attn_grp = keep.tile([P, PASSES_1 * P, PACK], BF16, name="attn_grp", align_bytes=64)
        nc.scalar.copy(
            out=attn_grp[:]
            .rearrange("p r t -> p (r t)")
            .bitcast(F32)
            .rearrange("p (g r u) -> p g r u", g=PASSES_1, u=2),
            in_=attnT_ps[:].rearrange("p g u r -> p g r u"),
        )
        quantise_w_out(0)

        regroup_on_vector(nc, wo_grp[1], wo_raw[1], VECTOR_COLS_WO[1])
        regroup_on_scalar(nc, wo_grp[1], wo_raw[1], VECTOR_COLS_WO[1])
        attn_codes = keep.tile([P, PASSES_1 * P], U32, name="attn_codes", align_bytes=64)
        attn_scales = keep.tile([P, PASSES_1 * P], U8, name="attn_scales", align_bytes=64)
        quantise(nc, attn_codes[:], attn_scales[:], attn_grp[:])
        quantise_w_out(1)

        vecT_ps = psum.tile([P, P], BF16, tag="bank", name="vecT_ps")
        nc.tensor.transpose(vecT_ps[:], vec_rows[:], ident_bf16[:])
        ln_cols = keep.tile([P, 2 * D_ROWS], BF16, name="ln_cols")
        nc.scalar.copy(out=ln_cols[:], in_=vecT_ps[:, G_ROW:P])

        xb_ps = psum.tile([P, D], F32, tag="bank", name="xb_ps")
        nc.tensor.matmul(xb_ps[:], lhsT=ones_bf16[:], rhs=bias_rows[:], start=True, stop=False)
        nc.tensor.matmul(xb_ps[:], lhsT=ident_bf16[:], rhs=x_sb[:], start=False, stop=True)
        xb_sb = keep.tile([P, D], F32, name="xb_sb")
        nc.scalar.copy(out=xb_sb[:], in_=xb_ps[:])

        halves = [slice(h * (D // 2), (h + 1) * (D // 2)) for h in range(2)]
        acc1_ps = [psum.tile([P, D // 2], F32, tag="bank", name="acc1_ps%d" % h) for h in range(2)]
        for g in range(PASSES_1):
            tokens = slice(g * P, (g + 1) * P)
            for h, half in enumerate(halves):
                nc.tensor.matmul_mx(
                    out=acc1_ps[h][:],
                    lhsT=attn_codes[:, tokens].bitcast(FP8X4),
                    lhsT_scale=attn_scales[:, tokens],
                    rhs=wo_codes[:, g, half].bitcast(FP8X4),
                    rhs_scale=wo_scales[:, g, half],
                    start=(g == 0),
                    stop=(g == PASSES_1 - 1),
                )
        regroup_on_vector(nc, w1_grp[0], w1_raw[0], VECTOR_COLS_W1[0])
        one = keep.tile([P, 1], F32, name="one")
        nc.vector.memset(one[:], 1.0)
        regroup_on_gpsimd(nc, w1_grp[0], w1_raw[0], VECTOR_COLS_W1[0], one[:])
        regroup_on_scalar(nc, w1_grp[1], w1_raw[1], VECTOR_COLS_W1[1])
        x_mid = keep.tile([P, D], F32, name="x_mid")
        for h, half in enumerate(halves):
            nc.vector.tensor_tensor(
                out=x_mid[:, half], in0=acc1_ps[h][:], in1=xb_sb[:, half], op=ALU.add
            )
        nc.sync.dma_start(out=out_0.rearrange("b t d -> (b t) d"), in_=x_mid[:])

        ln_ps = psum.tile([P, 2, D], BF16, tag="bank", name="ln_ps")
        for r in range(2 * D_ROWS):
            first = (r % D_ROWS) * P
            nc.tensor.transpose(
                ln_ps[:, r // D_ROWS, first : first + P],
                ln_cols[:, r : r + 1].to_broadcast([P, P]),
                ident_bf16[:],
            )
        regroup_on_scalar(nc, w1_grp[2], w1_raw[2], VECTOR_COLS_W1[2])

        stats = keep.tile([P, 2, 6], F32, name="stats")
        for h, half in enumerate(halves):
            nc.vector.bn_stats(out=stats[:, h, :], in_=x_mid[:, half])
        regroup_on_vector(nc, w1_grp[1], w1_raw[1], VECTOR_COLS_W1[1])
        mean_var = keep.tile([P, 2], F32, name="mean_var")
        nc.vector.bn_aggr(out=mean_var[:], in_=stats[:])
        var_eps = keep.tile([P, 1], F32, name="var_eps")
        nc.vector.tensor_scalar_add(out=var_eps[:], in0=mean_var[:, 1:2], scalar1=EPS)
        rstd = keep.tile([P, 1], F32, name="rstd")
        nc.gpsimd.tensor_tensor(out=rstd[:], in0=var_eps[:], in1=neg_half[:], op=ALU.pow)
        centred = keep.tile([P, D], F32, name="centred")
        nc.vector.scalar_tensor_tensor(
            out=centred[:],
            in0=x_mid[:],
            scalar=mean_var[:, 0:1],
            in1=ln_ps[:, 0, :],
            op0=ALU.subtract,
            op1=ALU.mult,
        )
        quantise_w1(0)

        h2 = keep.tile([P, D], BF16, name="h2")
        nc.vector.scalar_tensor_tensor(
            out=h2[:],
            in0=centred[:],
            scalar=rstd[:],
            in1=ln_ps[:, 1, :],
            op0=ALU.mult,
            op1=ALU.add,
        )
        h2_words = h2[:].bitcast(F32)
        h2T_ps = psum.tile([P, 2, P], F32, tag="bank", name="h2T_ps")
        for u in range(2):
            nc.tensor.transpose(h2T_ps[:, u, :], h2_words[:, slice(u, 2 * P, 2)], ident_f32[:])
        regroup_on_vector(nc, w1_grp[2], w1_raw[2], VECTOR_COLS_W1[2])
        quantise_w1(1)
        h2_grp = keep.tile([P, P, PACK], BF16, name="h2_grp", align_bytes=64)
        nc.vector.tensor_copy(
            out=h2_grp[:]
            .rearrange("p r t -> p (r t)")
            .bitcast(F32)
            .rearrange("p (r u) -> p r u", u=2),
            in_=h2T_ps[:].rearrange("p u r -> p r u"),
        )
        regroup_on_scalar(nc, w1_grp[3], w1_raw[3], VECTOR_COLS_W1[3])
        regroup_on_vector(nc, w1_grp[3], w1_raw[3], VECTOR_COLS_W1[3])
        h2_codes = keep.tile([P, P], U32, name="h2_codes", align_bytes=64)
        h2_scales = keep.tile([P, P], U8, name="h2_scales", align_bytes=64)
        quantise(nc, h2_codes[:], h2_scales[:], h2_grp[:])

        hid_rows = out_1.rearrange("b t f -> (b t) f")
        def multiply(c, parts):
            width = CHUNK // parts
            banks = []
            for i in range(parts):
                cols = slice(i * width, (i + 1) * width)
                bank = psum.tile([P, width], F32, tag="bank", name="hid_ps%d_%d" % (c, i))
                nc.tensor.matmul_mx(
                    out=bank[:],
                    lhsT=h2_codes[:].bitcast(FP8X4),
                    lhsT_scale=h2_scales[:],
                    rhs=w1_codes[:, c, cols].bitcast(FP8X4),
                    rhs_scale=w1_scales[:, c, cols],
                    start=True,
                    stop=True,
                )
                banks.append((c * CHUNK + i * width, width, bank))
            return banks

        def finish(first, width, bank):
            feats = slice(first, first + width)
            pre = keep.tile([P, width], F32, name="pre%d" % first)
            nc.vector.tensor_tensor(out=pre[:], in0=bank[:], in1=b1_all[:, feats], op=ALU.add)
            hid_sb = keep.tile([P, width], F32, name="hid_sb%d" % first)
            nc.scalar.activation(out=hid_sb[:], in_=pre[:], func=ACT.Gelu)
            nc.sync.dma_start(out=hid_rows[:, feats], in_=hid_sb[:])

        parts_of = [2, 1, 1, 2]
        products = [multiply(c, parts_of[c]) for c in range(2)]
        quantise_w1(2)
        products.append(multiply(2, parts_of[2]))
        for part in products[0]:
            finish(*part)
        quantise_w1(3)
        products.append(multiply(3, parts_of[3]))
        for product in products[1:]:
            for part in product:
                finish(*part)
